import numpy as np
import ml_dtypes


def mxq(x, axis, fmt="e4m3"):
    dtype, down = {"e4m3": (ml_dtypes.float8_e4m3fn, 7), "e5m2": (ml_dtypes.float8_e5m2, 14)}[fmt]
    v = np.moveaxis(np.asarray(x, np.float32).astype(ml_dtypes.bfloat16).astype(np.float64), axis, -1)
    blocks = v.reshape(v.shape[:-1] + (-1, 32))
    amax = np.abs(blocks).max(-1, keepdims=True)
    byte = np.maximum(np.where(amax > 0, np.frexp(amax)[1] - 1 + 127, 0) - down, 1)
    scale = np.exp2(byte - 127.0)
    codes = (blocks / scale).astype(np.float32).astype(dtype).astype(np.float64)
    return np.moveaxis((codes * scale).reshape(v.shape), -1, axis)


WIDE = False


def mx_kscale(k):
    if not WIDE:
        return np.ones(k)
    levels = np.array([10, -10, 5, -5, 0])
    if k % 512:
        return np.exp2(np.random.permutation(np.resize(levels, k // 32))).repeat(32)
    a = np.empty((k // 512, 16))
    for p in range(k // 512):
        a[p, :8] = np.random.permutation(np.resize(levels, 8))
        for g in range(8):
            far = levels[np.abs(levels - a[p, g]) >= 10]
            a[p, g + 8] = far[np.random.randint(len(far))]
    return np.exp2(a.ravel()).repeat(32)


BF16 = ml_dtypes.bfloat16


def bf(x):
    return np.asarray(x, np.float32).astype(BF16)


def f64(x):
    return np.asarray(x).astype(np.float64)


G, GI, GO, B = 32, 32, 32, 4096
K = G * GI
N = G * GO


def block_gain():
    gain = np.ones((N, K))
    for g in range(G):
        gain[g * GO:(g + 1) * GO, g * GI:(g + 1) * GI] = 0.5
    return gain


def setup_inputs():
    s = mx_kscale(K)
    bound = 1.0 / np.sqrt(K)
    W = np.random.uniform(-bound, bound, (N, K)) * block_gain()
    return {"data": bf(np.random.standard_normal((B, K)) * s),
            "W": bf(W / s[None, :]),
            "b": bf(np.random.standard_normal(N) * 0.3)}


def core(data, W, b):
    return (mxq(f64(data), 1, "e4m3") @ mxq(f64(W), 1, "e4m3").T) + f64(b)


def e4m3fn_bytes(y):
    return np.clip(np.asarray(y, np.float64), -448.0, 448.0).astype(np.float32).astype(ml_dtypes.float8_e4m3fn).view(np.uint8)


Y_SCALE = 340.0


def reference(data, W, b):
    out = core(data, W, b)
    return out, e4m3fn_bytes(out * Y_SCALE)

@@ -1,0 +1,195 @@
+from contextlib import ExitStack
+
+import concourse.mybir as mybir
+from concourse.masks import make_identity
+
+B, K, N = 4096, 1024, 1024
+FLOPS = 2 * B * K * N
+Y_SCALE = 340.0
+
+F32 = mybir.dt.float32
+BF16 = mybir.dt.bfloat16
+U32 = mybir.dt.uint32
+U8 = mybir.dt.uint8
+FP8X4 = mybir.dt.float8_e4m3fn_x4
+FP8 = mybir.dt.float8_e4m3fn
+ADD = mybir.AluOpType.add
+COPY = mybir.ActivationFunctionType.Copy
+
+P = 128
+G = 2
+H = 2
+J = 4
+S = B // (P * J)
+NT = S * J
+WT = N // P
+R = 2
+E_ON_VECTOR = (3,)
+
+
+def tile_groupfc_kernel(tc, data, W, b, out_0, out_1):
+    nc = tc.nc
+    data_v = data.rearrange("(s p j) k -> s p j k", p=P, j=J)
+    out0_v = out_0.rearrange("(s p j) n -> s p j n", p=P, j=J)
+    out1_v = out_1.rearrange("(s p j) n -> s p (j n)", p=P, j=J)
+    w_v = W.rearrange("(t p) k -> t p k", p=P)
+
+    with ExitStack() as ctx:
+        const = ctx.enter_context(tc.tile_pool(name="const", bufs=1))
+        raw = ctx.enter_context(tc.tile_pool(name="raw", bufs=1))
+        grp = ctx.enter_context(tc.tile_pool(name="grp", bufs=4))
+        cod = ctx.enter_context(tc.tile_pool(name="cod", bufs=6))
+        outp = ctx.enter_context(tc.tile_pool(name="outp", bufs=4))
+        out8 = ctx.enter_context(tc.tile_pool(name="out8", bufs=3))
+        psum_t = ctx.enter_context(tc.psum_pool(name="psum_t", bufs=4))
+        psum_o = ctx.enter_context(tc.psum_pool(name="psum_o", bufs=4))
+
+        ident = const.tile([P, P], F32, name="ident")
+        make_identity(nc, ident[:])
+        ones = const.tile([P, P], BF16, name="ones")
+        b_row = const.tile([P, N], BF16, name="b_row")
+        bias = const.tile([P, N], F32, name="bias")
+        w_codes = const.tile([P, G, N], U32, name="w_codes", align_bytes=64)
+        w_scales = const.tile([P, G, N], U8, name="w_scales", align_bytes=64)
+
+        ctx.enter_context(tc.manual_schedule())
+
+        nc.vector.memset(ones[:], 1.0)
+        nc.vector.memset(b_row[:], 0.0)
+
+        w_raw = []
+        for t in range(WT):
+            wr = raw.tile([P, K], BF16, name="w_raw%d" % t)
+            nc.sync.dma_start(out=wr[:], in_=w_v[t])
+            w_raw.append(wr)
+        x_raw = []
+        for s in range(S):
+            xr = raw.tile([P, J, K], BF16, name="x_raw%d" % s)
+            x_raw.append(xr)
+        for j in range(J):
+            nc.sync.dma_start(out=x_raw[0][:, j, :], in_=data_v[0][:, j, :])
+        nc.sync.dma_start(out=b_row[0:1, :], in_=b.rearrange("(o n) -> o n", o=1))
+        for s in range(1, S):
+            nc.sync.dma_start(out=x_raw[s][:], in_=data_v[s])
+
+        def transposes(rows):
+            words = rows.bitcast(F32)
+            tp = psum_t.tile([P, G, 2, P], F32, name="tp")
+            for g in range(G):
+                for u in range(2):
+                    nc.tensor.transpose(tp[:, g, u, :], words[:, 256 * g + u:256 * (g + 1):2], ident[:])
+            return tp
+
+        def copy_out(tp, on_vector):
+            gr = grp.tile([P, G, P, 4], BF16, name="gr", align_bytes=64)
+            dst = gr[:].bitcast(F32)
+            src = tp[:].rearrange("p g u r -> p g r u")
+            if on_vector:
+                nc.vector.tensor_copy(out=dst, in_=src)
+            else:
+                nc.scalar.copy(out=dst, in_=src)
+            return gr
+
+        for t in range(WT):
+            tp = transposes(w_raw[t][:])
+            gr = copy_out(tp, False)
+            for g in range(G):
+                cols = slice(t * P, (t + 1) * P)
+                nc.vector.quantize_mx(
+                    out=w_codes[:, g, cols].bitcast(FP8X4),
+                    scales=w_scales[:, g, cols],
+                    in_=gr[:, g, :, :].rearrange("p r t -> p (r t)"),
+                )
+
+        tps = {}
+        grs = {}
+        cds = {}
+        pos = {}
+        o_t = {}
+        o8_t = {}
+
+        def t_step(i):
+            tps[i] = transposes(x_raw[i // J][:, i % J, :])
+
+        def e_step(i):
+            grs[i] = copy_out(tps.pop(i), (i % 4) in E_ON_VECTOR)
+
+        def q_step(i):
+            codes = cod.tile([P, G * P], U32, name="codes", align_bytes=64)
+            scales = cod.tile([P, G * P], U8, name="scales", align_bytes=64)
+            nc.vector.quantize_mx(
+                out=codes[:].bitcast(FP8X4),
+                scales=scales[:],
+                in_=grs.pop(i)[:].rearrange("p g r t -> p (g r t)"),
+            )
+            cds[i] = (codes, scales)
+
+        def m_step(i):
+            codes, scales = cds.pop(i)
+            banks = []
+            for h in range(H):
+                po = psum_o.tile([P, 512], F32, name="po")
+                for g in range(G):
+                    nc.tensor.matmul_mx(
+                        out=po[:],
+                        lhsT=codes[:, g * P:(g + 1) * P].bitcast(FP8X4),
+                        lhsT_scale=scales[:, g * P:(g + 1) * P],
+                        rhs=w_codes[:, g, h * 512:(h + 1) * 512].bitcast(FP8X4),
+                        rhs_scale=w_scales[:, g, h * 512:(h + 1) * 512],
+                        start=(g == 0),
+                        stop=(g == G - 1),
+                    )
+                banks.append(po)
+            pos[i] = banks
+
+        def b_step(i):
+            s, j = i // J, i % J
+            if j == 0:
+                o_t[s] = outp.tile([P, J, N], F32, name="o")
+            banks = pos.pop(i)
+            for h in range(H):
+                cols = slice(h * 512, (h + 1) * 512)
+                nc.vector.tensor_tensor(out=o_t[s][:, j, cols], in0=banks[h][:], in1=bias[:, cols], op=ADD)
+            if j == J - 1:
+                nc.sync.dma_start(out=out0_v[s], in_=o_t[s][:])
+
+        def c_step(i):
+            s, j = i // J, i % J
+            if j == 0:
+                o8_t[s] = out8.tile([P, J, N], FP8, name="o8")
+            nc.scalar.activation(out=o8_t[s][:, j, :], in_=o_t[s][:, j, :], func=COPY, scale=Y_SCALE, saturate=False)
+            if j == J - 1:
+                nc.sync.dma_start(out=out1_v[s], in_=o8_t[s][:].rearrange("p j n -> p (j n)").bitcast(U8))
+
+        for i in range(R):
+            t_step(i)
+        for h in range(H):
+            cols = slice(h * 512, (h + 1) * 512)
+            pb = psum_o.tile([P, 512], F32, name="po")
+            nc.tensor.matmul(out=pb[:], lhsT=ones[:], rhs=b_row[:, cols], start=True, stop=True)
+            nc.vector.tensor_copy(out=bias[:, cols], in_=pb[:])
+        for i in range(R):
+            e_step(i)
+        for i in range(R):
+            q_step(i)
+
+        for k in range(NT // R + 1):
+            bb = k * R
+            aa = bb + R
+            nxt = [i for i in range(aa, aa + R) if i < NT]
+            cur = [i for i in range(bb, bb + R) if i < NT]
+            for i in nxt:
+                t_step(i)
+            if bb > 0:
+                b_step(bb - 1)
+            for i in nxt:
+                e_step(i)
+            for i in nxt:
+                q_step(i)
+            for i in cur:
+                m_step(i)
+                if i != cur[-1]:
+                    b_step(i)
+            for i in range(bb - R, bb):
+                if i >= 0:
+                    c_step(i)

@@ -19,19 +19,22 @@ COPY = mybir.ActivationFunctionType.Copy
 P = 128
 G = 2
 H = 2
+JL = 8
 J = 4
-S = B // (P * J)
-NT = S * J
+NT = B // P
 WT = N // P
 R = 2
 E_ON_VECTOR = (3,)
+STORE0 = (4, 4, 4, 4, 2, 2, 2, 1)
+STORE1 = (4, 4, 4, 4, 4, 4, 2, 1)
+FIRST_LOADS = ((0, 1), (1, 2), (2, 4), (4, 8))
 
 
 def tile_groupfc_kernel(tc, data, W, b, out_0, out_1):
     nc = tc.nc
-    data_v = data.rearrange("(s p j) k -> s p j k", p=P, j=J)
-    out0_v = out_0.rearrange("(s p j) n -> s p j n", p=P, j=J)
-    out1_v = out_1.rearrange("(s p j) n -> s p (j n)", p=P, j=J)
+    data_v = data.rearrange("(s p j) k -> s p j k", p=P, j=JL)
+    out0_v = out_0.rearrange("(s p j) n -> s p j n", p=P, j=JL)
+    out1_v = out_1.rearrange("(s p j) n -> s p j n", p=P, j=JL)
     w_v = W.rearrange("(t p) k -> t p k", p=P)
 
     with ExitStack() as ctx:
@@ -54,23 +57,25 @@ def tile_groupfc_kernel(tc, data, W, b, out_0, out_1):
 
         ctx.enter_context(tc.manual_schedule())
 
-        nc.vector.memset(ones[:], 1.0)
         nc.vector.memset(b_row[:], 0.0)
+        nc.vector.memset(ones[:], 1.0)
 
         w_raw = []
         for t in range(WT):
             wr = raw.tile([P, K], BF16, name="w_raw%d" % t)
             nc.sync.dma_start(out=wr[:], in_=w_v[t])
             w_raw.append(wr)
+            if t == 3:
+                nc.sync.dma_start(out=b_row[0:1, :], in_=b.rearrange("(o n) -> o n", o=1))
         x_raw = []
-        for s in range(S):
-            xr = raw.tile([P, J, K], BF16, name="x_raw%d" % s)
+        for s in range(NT // JL):
+            xr = raw.tile([P, JL, K], BF16, name="x_raw%d" % s)
             x_raw.append(xr)
-        for j in range(J):
-            nc.sync.dma_start(out=x_raw[0][:, j, :], in_=data_v[0][:, j, :])
-        nc.sync.dma_start(out=b_row[0:1, :], in_=b.rearrange("(o n) -> o n", o=1))
-        for s in range(1, S):
-            nc.sync.dma_start(out=x_raw[s][:], in_=data_v[s])
+            if s == 0:
+                for j0, j1 in FIRST_LOADS:
+                    nc.sync.dma_start(out=xr[:, j0:j1, :], in_=data_v[0][:, j0:j1, :])
+            else:
+                nc.sync.dma_start(out=xr[:], in_=data_v[s])
 
         def transposes(rows):
             words = rows.bitcast(F32)
@@ -101,6 +106,12 @@ def tile_groupfc_kernel(tc, data, W, b, out_0, out_1):
                     in_=gr[:, g, :, :].rearrange("p r t -> p (r t)"),
                 )
 
+        for h in range(H):
+            cols = slice(h * 512, (h + 1) * 512)
+            pb = psum_o.tile([P, 512], F32, name="po")
+            nc.tensor.matmul(out=pb[:], lhsT=ones[:], rhs=b_row[:, cols], start=True, stop=True)
+            nc.vector.tensor_copy(out=bias[:, cols], in_=pb[:])
+
         tps = {}
         grs = {}
         cds = {}
@@ -109,7 +120,7 @@ def tile_groupfc_kernel(tc, data, W, b, out_0, out_1):
         o8_t = {}
 
         def t_step(i):
-            tps[i] = transposes(x_raw[i // J][:, i % J, :])
+            tps[i] = transposes(x_raw[i // JL][:, i % JL, :])
 
         def e_step(i):
             grs[i] = copy_out(tps.pop(i), (i % 4) in E_ON_VECTOR)
@@ -143,35 +154,46 @@ def tile_groupfc_kernel(tc, data, W, b, out_0, out_1):
             pos[i] = banks
 
         def b_step(i):
-            s, j = i // J, i % J
+            q, j = i // J, i % J
             if j == 0:
-                o_t[s] = outp.tile([P, J, N], F32, name="o")
+                o_t[q] = outp.tile([P, J, N], F32, name="o")
             banks = pos.pop(i)
             for h in range(H):
                 cols = slice(h * 512, (h + 1) * 512)
-                nc.vector.tensor_tensor(out=o_t[s][:, j, cols], in0=banks[h][:], in1=bias[:, cols], op=ADD)
-            if j == J - 1:
-                nc.sync.dma_start(out=out0_v[s], in_=o_t[s][:])
+                nc.vector.tensor_tensor(out=o_t[q][:, j, cols], in0=banks[h][:], in1=bias[:, cols], op=ADD)
+            w = STORE0[q]
+            if (j + 1) % w == 0:
+                j8 = i % JL
+                nc.sync.dma_start(out=out0_v[i // JL][:, j8 - w + 1:j8 + 1, :], in_=o_t[q][:, j - w + 1:j + 1, :])
 
         def c_step(i):
-            s, j = i // J, i % J
+            q, j = i // J, i % J
             if j == 0:
-                o8_t[s] = out8.tile([P, J, N], FP8, name="o8")
-            nc.scalar.activation(out=o8_t[s][:, j, :], in_=o_t[s][:, j, :], func=COPY, scale=Y_SCALE, saturate=False)
-            if j == J - 1:
-                nc.sync.dma_start(out=out1_v[s], in_=o8_t[s][:].rearrange("p j n -> p (j n)").bitcast(U8))
+                o8_t[q] = out8.tile([P, J, N], FP8, name="o8")
+            nc.scalar.activation(out=o8_t[q][:, j, :], in_=o_t[q][:, j, :], func=COPY, scale=Y_SCALE, saturate=False)
+            w = STORE1[q]
+            if (j + 1) % w == 0:
+                j8 = i % JL
+                nc.sync.dma_start(
+                    out=out1_v[i // JL][:, j8 - w + 1:j8 + 1, :].rearrange("p j n -> p (j n)"),
+                    in_=o8_t[q][:, j - w + 1:j + 1, :].rearrange("p j n -> p (j n)").bitcast(U8),
+                )
 
         for i in range(R):
             t_step(i)
-        for h in range(H):
-            cols = slice(h * 512, (h + 1) * 512)
-            pb = psum_o.tile([P, 512], F32, name="po")
-            nc.tensor.matmul(out=pb[:], lhsT=ones[:], rhs=b_row[:, cols], start=True, stop=True)
-            nc.vector.tensor_copy(out=bias[:, cols], in_=pb[:])
         for i in range(R):
             e_step(i)
         for i in range(R):
             q_step(i)
+
+        casts = [0]
+
+        def casts_up_to(last, at_most):
+            n = 0
+            while casts[0] <= last and n < at_most:
+                c_step(casts[0])
+                casts[0] += 1
+                n += 1
 
         for k in range(NT // R + 1):
             bb = k * R
@@ -187,9 +209,11 @@ def tile_groupfc_kernel(tc, data, W, b, out_0, out_1):
             for i in nxt:
                 q_step(i)
             for i in cur:
+                casts_up_to(bb - 1, 1)
                 m_step(i)
                 if i != cur[-1]:
                     b_step(i)
-            for i in range(bb - R, bb):
-                if i >= 0:
-                    c_step(i)
+            if nxt or not cur:
+                casts_up_to(bb - 1, NT)
+            else:
+                casts_up_to(cur[-1] - 1, NT)

@@ -22,12 +22,22 @@ H = 2
 JL = 8
 J = 4
 NT = B // P
-WT = N // P
+WQ = 4
+WARM = 5
 R = 2
 E_ON_VECTOR = (3,)
-STORE0 = (4, 4, 4, 4, 2, 2, 2, 1)
-STORE1 = (4, 4, 4, 4, 4, 4, 2, 1)
-FIRST_LOADS = ((0, 1), (1, 2), (2, 4), (4, 8))
+STORE0 = ((4,), (4,), (4,), (4,), (4,), (2, 2), (2, 2), (1, 1, 1, 1))
+STORE1 = ((4,), (4,), (4,), (4,), (4,), (4,), (2, 2), (2, 1, 1))
+FIRST_LOADS = ((0, 2), (2, 4), (4, 8))
+
+
+def store_width(pattern, j):
+    first = 0
+    for w in pattern:
+        if j == first + w - 1:
+            return w
+        first += w
+    return 0
 
 
 def tile_groupfc_kernel(tc, data, W, b, out_0, out_1):
@@ -35,7 +45,7 @@ def tile_groupfc_kernel(tc, data, W, b, out_0, out_1):
     data_v = data.rearrange("(s p j) k -> s p j k", p=P, j=JL)
     out0_v = out_0.rearrange("(s p j) n -> s p j n", p=P, j=JL)
     out1_v = out_1.rearrange("(s p j) n -> s p j n", p=P, j=JL)
-    w_v = W.rearrange("(t p) k -> t p k", p=P)
+    w_v = W.rearrange("(q p t) k -> q p t k", p=P, t=2)
 
     with ExitStack() as ctx:
         const = ctx.enter_context(tc.tile_pool(name="const", bufs=1))
@@ -50,6 +60,7 @@ def tile_groupfc_kernel(tc, data, W, b, out_0, out_1):
         ident = const.tile([P, P], F32, name="ident")
         make_identity(nc, ident[:])
         ones = const.tile([P, P], BF16, name="ones")
+        warm = const.tile([P, 512], BF16, name="warm")
         b_row = const.tile([P, N], BF16, name="b_row")
         bias = const.tile([P, N], F32, name="bias")
         w_codes = const.tile([P, G, N], U32, name="w_codes", align_bytes=64)
@@ -57,15 +68,16 @@ def tile_groupfc_kernel(tc, data, W, b, out_0, out_1):
 
         ctx.enter_context(tc.manual_schedule())
 
-        nc.vector.memset(b_row[:], 0.0)
         nc.vector.memset(ones[:], 1.0)
+        nc.vector.memset(warm[:], 0.0)
+        nc.vector.memset(b_row[:], 0.0)
 
         w_raw = []
-        for t in range(WT):
-            wr = raw.tile([P, K], BF16, name="w_raw%d" % t)
-            nc.sync.dma_start(out=wr[:], in_=w_v[t])
+        for q in range(WQ):
+            wr = raw.tile([P, 2, K], BF16, name="w_raw%d" % q)
+            nc.sync.dma_start(out=wr[:], in_=w_v[q])
             w_raw.append(wr)
-            if t == 3:
+            if q == 1:
                 nc.sync.dma_start(out=b_row[0:1, :], in_=b.rearrange("(o n) -> o n", o=1))
         x_raw = []
         for s in range(NT // JL):
@@ -95,15 +107,28 @@ def tile_groupfc_kernel(tc, data, W, b, out_0, out_1):
                 nc.scalar.copy(out=dst, in_=src)
             return gr
 
-        for t in range(WT):
-            tp = transposes(w_raw[t][:])
-            gr = copy_out(tp, False)
+        pw = psum_o.tile([P, 512], F32, name="po")
+        for n in range(WARM):
+            nc.tensor.matmul(out=pw[:], lhsT=ones[:], rhs=warm[:], start=True, stop=True)
+
+        for q in range(WQ):
             for g in range(G):
-                cols = slice(t * P, (t + 1) * P)
+                tp = psum_t.tile([P, 2, 2, P], F32, name="tp")
+                for t in range(2):
+                    words = w_raw[q][:, t, :].bitcast(F32)
+                    for u in range(2):
+                        nc.tensor.transpose(tp[:, t, u, :], words[:, 256 * g + u:256 * (g + 1):2], ident[:])
+                gr = grp.tile([P, G, P, 4], BF16, name="gr", align_bytes=64)
+                flat = gr[:].rearrange("p a r c -> p (a r c)")
+                nc.scalar.copy(
+                    out=flat.bitcast(F32).rearrange("p (r t u) -> p r t u", t=2, u=2),
+                    in_=tp[:].rearrange("p t u r -> p r t u"),
+                )
+                cols = slice(q * 256, (q + 1) * 256)
                 nc.vector.quantize_mx(
                     out=w_codes[:, g, cols].bitcast(FP8X4),
                     scales=w_scales[:, g, cols],
-                    in_=gr[:, g, :, :].rearrange("p r t -> p (r t)"),
+                    in_=flat,
                 )
 
         for h in range(H):
@@ -161,8 +186,8 @@ def tile_groupfc_kernel(tc, data, W, b, out_0, out_1):
             for h in range(H):
                 cols = slice(h * 512, (h + 1) * 512)
                 nc.vector.tensor_tensor(out=o_t[q][:, j, cols], in0=banks[h][:], in1=bias[:, cols], op=ADD)
-            w = STORE0[q]
-            if (j + 1) % w == 0:
+            w = store_width(STORE0[q], j)
+            if w:
                 j8 = i % JL
                 nc.sync.dma_start(out=out0_v[i // JL][:, j8 - w + 1:j8 + 1, :], in_=o_t[q][:, j - w + 1:j + 1, :])
 
@@ -170,9 +195,14 @@ def tile_groupfc_kernel(tc, data, W, b, out_0, out_1):
             q, j = i // J, i % J
             if j == 0:
                 o8_t[q] = out8.tile([P, J, N], FP8, name="o8")
-            nc.scalar.activation(out=o8_t[q][:, j, :], in_=o_t[q][:, j, :], func=COPY, scale=Y_SCALE, saturate=False)
-            w = STORE1[q]
-            if (j + 1) % w == 0:
+            pieces = H if i == NT - 1 else 1
+            for c in range(pieces):
+                cols = slice(c * N // pieces, (c + 1) * N // pieces)
+                nc.scalar.activation(
+                    out=o8_t[q][:, j, cols], in_=o_t[q][:, j, cols], func=COPY, scale=Y_SCALE, saturate=False
+                )
+            w = store_width(STORE1[q], j)
+            if w:
                 j8 = i % JL
                 nc.sync.dma_start(
                     out=out1_v[i // JL][:, j8 - w + 1:j8 + 1, :].rearrange("p j n -> p (j n)"),

@@ -186,15 +186,22 @@ def tile_groupfc_kernel(tc, data, W, b, out_0, out_1):
             for h in range(H):
                 cols = slice(h * 512, (h + 1) * 512)
                 nc.vector.tensor_tensor(out=o_t[q][:, j, cols], in0=banks[h][:], in1=bias[:, cols], op=ADD)
+            if q == NT // J - 1:
+                store0(nc.sync, i)
+
+        def store0(queue, i):
+            q, j = i // J, i % J
             w = store_width(STORE0[q], j)
             if w:
                 j8 = i % JL
-                nc.sync.dma_start(out=out0_v[i // JL][:, j8 - w + 1:j8 + 1, :], in_=o_t[q][:, j - w + 1:j + 1, :])
+                queue.dma_start(out=out0_v[i // JL][:, j8 - w + 1:j8 + 1, :], in_=o_t[q][:, j - w + 1:j + 1, :])
 
         def c_step(i):
             q, j = i // J, i % J
             if j == 0:
                 o8_t[q] = out8.tile([P, J, N], FP8, name="o8")
+            if q < NT // J - 1:
+                store0(nc.scalar, i)
             pieces = H if i == NT - 1 else 1
             for c in range(pieces):
                 cols = slice(c * N // pieces, (c + 1) * N // pieces)

@@ -25,7 +25,7 @@ NT = B // P
 WQ = 4
 WARM = 5
 R = 2
-E_ON_VECTOR = (3,)
+E_ON_VECTOR = ()
 STORE0 = ((4,), (4,), (4,), (4,), (4,), (2, 2), (2, 2), (1, 1, 1, 1))
 STORE1 = ((4,), (4,), (4,), (4,), (4,), (4,), (2, 2), (2, 1, 1))
 FIRST_LOADS = ((0, 2), (2, 4), (4, 8))

@@ -24,9 +24,9 @@ J = 4
 NT = B // P
 WQ = 4
 WARM = 5
-R = 2
-E_ON_VECTOR = ()
-STORE0 = ((4,), (4,), (4,), (4,), (4,), (2, 2), (2, 2), (1, 1, 1, 1))
+GROUPS = (4, 4, 4, 4, 4, 4, 4, 2, 2)
+LAG = 2
+STORE0 = ((2, 2), (2, 2), (2, 2), (2, 2), (2, 2), (2, 2), (2, 2), (1, 1, 1, 1))
 STORE1 = ((4,), (4,), (4,), (4,), (4,), (4,), (2, 2), (2, 1, 1))
 FIRST_LOADS = ((0, 2), (2, 4), (4, 8))
 
@@ -50,12 +50,11 @@ def tile_groupfc_kernel(tc, data, W, b, out_0, out_1):
     with ExitStack() as ctx:
         const = ctx.enter_context(tc.tile_pool(name="const", bufs=1))
         raw = ctx.enter_context(tc.tile_pool(name="raw", bufs=1))
-        grp = ctx.enter_context(tc.tile_pool(name="grp", bufs=4))
-        cod = ctx.enter_context(tc.tile_pool(name="cod", bufs=6))
+        grp = ctx.enter_context(tc.tile_pool(name="grp", bufs=6))
+        cod = ctx.enter_context(tc.tile_pool(name="cod", bufs=10))
         outp = ctx.enter_context(tc.tile_pool(name="outp", bufs=4))
         out8 = ctx.enter_context(tc.tile_pool(name="out8", bufs=3))
-        psum_t = ctx.enter_context(tc.psum_pool(name="psum_t", bufs=4))
-        psum_o = ctx.enter_context(tc.psum_pool(name="psum_o", bufs=4))
+        psum = ctx.enter_context(tc.psum_pool(name="psum", bufs=8))
 
         ident = const.tile([P, P], F32, name="ident")
         make_identity(nc, ident[:])
@@ -89,31 +88,13 @@ def tile_groupfc_kernel(tc, data, W, b, out_0, out_1):
             else:
                 nc.sync.dma_start(out=xr[:], in_=data_v[s])
 
-        def transposes(rows):
-            words = rows.bitcast(F32)
-            tp = psum_t.tile([P, G, 2, P], F32, name="tp")
-            for g in range(G):
-                for u in range(2):
-                    nc.tensor.transpose(tp[:, g, u, :], words[:, 256 * g + u:256 * (g + 1):2], ident[:])
-            return tp
-
-        def copy_out(tp, on_vector):
-            gr = grp.tile([P, G, P, 4], BF16, name="gr", align_bytes=64)
-            dst = gr[:].bitcast(F32)
-            src = tp[:].rearrange("p g u r -> p g r u")
-            if on_vector:
-                nc.vector.tensor_copy(out=dst, in_=src)
-            else:
-                nc.scalar.copy(out=dst, in_=src)
-            return gr
-
-        pw = psum_o.tile([P, 512], F32, name="po")
+        pw = psum.tile([P, 512], F32, name="ps")
         for n in range(WARM):
             nc.tensor.matmul(out=pw[:], lhsT=ones[:], rhs=warm[:], start=True, stop=True)
 
         for q in range(WQ):
             for g in range(G):
-                tp = psum_t.tile([P, 2, 2, P], F32, name="tp")
+                tp = psum.tile([P, 2, 2, P], F32, name="ps")
                 for t in range(2):
                     words = w_raw[q][:, t, :].bitcast(F32)
                     for u in range(2):
@@ -133,7 +114,7 @@ def tile_groupfc_kernel(tc, data, W, b, out_0, out_1):
 
         for h in range(H):
             cols = slice(h * 512, (h + 1) * 512)
-            pb = psum_o.tile([P, 512], F32, name="po")
+            pb = psum.tile([P, 512], F32, name="ps")
             nc.tensor.matmul(out=pb[:], lhsT=ones[:], rhs=b_row[:, cols], start=True, stop=True)
             nc.vector.tensor_copy(out=bias[:, cols], in_=pb[:])
 
@@ -145,10 +126,17 @@ def tile_groupfc_kernel(tc, data, W, b, out_0, out_1):
         o8_t = {}
 
         def t_step(i):
-            tps[i] = transposes(x_raw[i // JL][:, i % JL, :])
+            words = x_raw[i // JL][:, i % JL, :].bitcast(F32)
+            tp = psum.tile([P, G, 2, P], F32, name="ps")
+            for g in range(G):
+                for u in range(2):
+                    nc.tensor.transpose(tp[:, g, u, :], words[:, 256 * g + u:256 * (g + 1):2], ident[:])
+            tps[i] = tp
 
         def e_step(i):
-            grs[i] = copy_out(tps.pop(i), (i % 4) in E_ON_VECTOR)
+            gr = grp.tile([P, G, P, 4], BF16, name="gr", align_bytes=64)
+            nc.scalar.copy(out=gr[:].bitcast(F32), in_=tps.pop(i)[:].rearrange("p g u r -> p g r u"))
+            grs[i] = gr
 
         def q_step(i):
             codes = cod.tile([P, G * P], U32, name="codes", align_bytes=64)
@@ -164,7 +152,7 @@ def tile_groupfc_kernel(tc, data, W, b, out_0, out_1):
             codes, scales = cds.pop(i)
             banks = []
             for h in range(H):
-                po = psum_o.tile([P, 512], F32, name="po")
+                po = psum.tile([P, 512], F32, name="ps")
                 for g in range(G):
                     nc.tensor.matmul_mx(
                         out=po[:],
@@ -186,22 +174,15 @@ def tile_groupfc_kernel(tc, data, W, b, out_0, out_1):
             for h in range(H):
                 cols = slice(h * 512, (h + 1) * 512)
                 nc.vector.tensor_tensor(out=o_t[q][:, j, cols], in0=banks[h][:], in1=bias[:, cols], op=ADD)
-            if q == NT // J - 1:
-                store0(nc.sync, i)
-
-        def store0(queue, i):
-            q, j = i // J, i % J
             w = store_width(STORE0[q], j)
             if w:
                 j8 = i % JL
-                queue.dma_start(out=out0_v[i // JL][:, j8 - w + 1:j8 + 1, :], in_=o_t[q][:, j - w + 1:j + 1, :])
+                nc.sync.dma_start(out=out0_v[i // JL][:, j8 - w + 1:j8 + 1, :], in_=o_t[q][:, j - w + 1:j + 1, :])
 
         def c_step(i):
             q, j = i // J, i % J
             if j == 0:
                 o8_t[q] = out8.tile([P, J, N], FP8, name="o8")
-            if q < NT // J - 1:
-                store0(nc.scalar, i)
             pieces = H if i == NT - 1 else 1
             for c in range(pieces):
                 cols = slice(c * N // pieces, (c + 1) * N // pieces)
@@ -216,41 +197,42 @@ def tile_groupfc_kernel(tc, data, W, b, out_0, out_1):
                     in_=o8_t[q][:, j - w + 1:j + 1, :].rearrange("p j n -> p (j n)").bitcast(U8),
                 )
 
-        for i in range(R):
-            t_step(i)
-        for i in range(R):
-            e_step(i)
-        for i in range(R):
-            q_step(i)
-
         casts = [0]
 
-        def casts_up_to(last, at_most):
-            n = 0
-            while casts[0] <= last and n < at_most:
+        def casts_to(last):
+            while casts[0] <= last:
                 c_step(casts[0])
                 casts[0] += 1
-                n += 1
 
-        for k in range(NT // R + 1):
-            bb = k * R
-            aa = bb + R
-            nxt = [i for i in range(aa, aa + R) if i < NT]
-            cur = [i for i in range(bb, bb + R) if i < NT]
+        runs = []
+        first = 0
+        for size in GROUPS:
+            runs.append(list(range(first, first + size)))
+            first += size
+        runs.append([])
+
+        for i in runs[0]:
+            t_step(i)
+        for i in runs[0]:
+            e_step(i)
+        for i in runs[0]:
+            q_step(i)
+
+        for r in range(len(GROUPS)):
+            cur = runs[r]
+            nxt = runs[r + 1]
             for i in nxt:
                 t_step(i)
-            if bb > 0:
-                b_step(bb - 1)
             for i in nxt:
                 e_step(i)
+            casts_to(cur[0] - 1)
             for i in nxt:
                 q_step(i)
+            held = LAG if nxt else 0
             for i in cur:
-                casts_up_to(bb - 1, 1)
                 m_step(i)
-                if i != cur[-1]:
-                    b_step(i)
-            if nxt or not cur:
-                casts_up_to(bb - 1, NT)
-            else:
-                casts_up_to(cur[-1] - 1, NT)
+                if i > cur[0]:
+                    b_step(i - 1)
+                    casts_to(min(i - 1, cur[-1] - held))
+            b_step(cur[-1])
+        casts_to(NT - 1)

@@ -24,7 +24,7 @@ J = 4
 NT = B // P
 WQ = 4
 WARM = 5
-GROUPS = (4, 4, 4, 4, 4, 4, 4, 2, 2)
+GROUPS = (2,) * 16
 LAG = 2
 STORE0 = ((2, 2), (2, 2), (2, 2), (2, 2), (2, 2), (2, 2), (2, 2), (1, 1, 1, 1))
 STORE1 = ((4,), (4,), (4,), (4,), (4,), (4,), (2, 2), (2, 1, 1))

@@ -153,9 +153,11 @@ def tile_groupfc_kernel(tc, data, W, b, out_0, out_1):
             banks = []
             for h in range(H):
                 po = psum.tile([P, 512], F32, name="ps")
-                for g in range(G):
+                banks.append(po)
+            for g in range(G):
+                for h in range(H):
                     nc.tensor.matmul_mx(
-                        out=po[:],
+                        out=banks[h][:],
                         lhsT=codes[:, g * P:(g + 1) * P].bitcast(FP8X4),
                         lhsT_scale=scales[:, g * P:(g + 1) * P],
                         rhs=w_codes[:, g, h * 512:(h + 1) * 512].bitcast(FP8X4),
@@ -163,7 +165,6 @@ def tile_groupfc_kernel(tc, data, W, b, out_0, out_1):
                         start=(g == 0),
                         stop=(g == G - 1),
                     )
-                banks.append(po)
             pos[i] = banks
 
         def b_step(i):

@@ -14,6 +14,7 @@ U8 = mybir.dt.uint8
 FP8X4 = mybir.dt.float8_e4m3fn_x4
 FP8 = mybir.dt.float8_e4m3fn
 ADD = mybir.AluOpType.add
+MULT = mybir.AluOpType.mult
 COPY = mybir.ActivationFunctionType.Copy
 
 P = 128
@@ -25,6 +26,7 @@ NT = B // P
 WQ = 4
 WARM = 5
 GROUPS = (2,) * 16
+DVE_CAST = 2
 LAG = 2
 STORE0 = ((2, 2), (2, 2), (2, 2), (2, 2), (2, 2), (2, 2), (2, 2), (1, 1, 1, 1))
 STORE1 = ((4,), (4,), (4,), (4,), (4,), (4,), (2, 2), (2, 1, 1))
@@ -184,11 +186,23 @@ def tile_groupfc_kernel(tc, data, W, b, out_0, out_1):
             q, j = i // J, i % J
             if j == 0:
                 o8_t[q] = out8.tile([P, J, N], FP8, name="o8")
-            pieces = H if i == NT - 1 else 1
-            for c in range(pieces):
-                cols = slice(c * N // pieces, (c + 1) * N // pieces)
+            scalar_cols = 0 if i % J == DVE_CAST else 512 if i == NT - 1 else N
+            if scalar_cols:
                 nc.scalar.activation(
-                    out=o8_t[q][:, j, cols], in_=o_t[q][:, j, cols], func=COPY, scale=Y_SCALE, saturate=False
+                    out=o8_t[q][:, j, :scalar_cols],
+                    in_=o_t[q][:, j, :scalar_cols],
+                    func=COPY,
+                    scale=Y_SCALE,
+                    saturate=False,
+                )
+            if scalar_cols < N:
+                nc.vector.tensor_scalar(
+                    out=o8_t[q][:, j, scalar_cols:],
+                    in0=o_t[q][:, j, scalar_cols:],
+                    scalar1=Y_SCALE,
+                    scalar2=None,
+                    op0=MULT,
+                    saturate=False,
                 )
             w = store_width(STORE1[q], j)
             if w:

@@ -27,6 +27,8 @@ WQ = 4
 WARM = 5
 GROUPS = (2,) * 16
 DVE_CAST = 2
+W_SORTED = False
+AFTER_W = ((("b", 0), ("b", 1)), (), (), ())
 LAG = 2
 STORE0 = ((2, 2), (2, 2), (2, 2), (2, 2), (2, 2), (2, 2), (2, 2), (1, 1, 1, 1))
 STORE1 = ((4,), (4,), (4,), (4,), (4,), (4,), (2, 2), (2, 1, 1))
@@ -69,16 +71,16 @@ def tile_groupfc_kernel(tc, data, W, b, out_0, out_1):
 
         ctx.enter_context(tc.manual_schedule())
 
+        nc.vector.memset(b_row[:].bitcast(F32), 0.0)
         nc.vector.memset(ones[:], 1.0)
-        nc.vector.memset(warm[:], 0.0)
-        nc.vector.memset(b_row[:], 0.0)
+        nc.vector.memset(warm[:].bitcast(F32), 0.0)
 
         w_raw = []
         for q in range(WQ):
             wr = raw.tile([P, 2, K], BF16, name="w_raw%d" % q)
             nc.sync.dma_start(out=wr[:], in_=w_v[q])
             w_raw.append(wr)
-            if q == 1:
+            if q == 0:
                 nc.sync.dma_start(out=b_row[0:1, :], in_=b.rearrange("(o n) -> o n", o=1))
         x_raw = []
         for s in range(NT // JL):
@@ -94,13 +96,45 @@ def tile_groupfc_kernel(tc, data, W, b, out_0, out_1):
         for n in range(WARM):
             nc.tensor.matmul(out=pw[:], lhsT=ones[:], rhs=warm[:], start=True, stop=True)
 
+        def w_sort(q):
+            ws = raw.tile([P, 2, G, 2, P], F32, name="w_srt%d" % q)
+            nc.vector.tensor_copy(
+                out=ws[:].rearrange("p t g u w -> p (t g) u w"),
+                in_=w_raw[q][:].rearrange("p t k -> p (t k)").bitcast(F32).rearrange("p (m w u) -> p m u w", m=2 * G, u=2),
+            )
+            return ws
+
+        def dummy(width):
+            pd = psum.tile([P, 512], F32, name="ps")
+            nc.tensor.matmul(out=pd[:, :width], lhsT=ones[:], rhs=warm[:, :width], start=True, stop=True)
+
+        pbs = []
+        bias_done = []
+
+        def bias_matmul(h):
+            pb = psum.tile([P, 512], F32, name="ps")
+            nc.tensor.matmul(out=pb[:], lhsT=ones[:], rhs=b_row[:, h * 512:(h + 1) * 512], start=True, stop=True)
+            pbs.append(pb)
+
+        w_srt = {}
+        if W_SORTED:
+            w_srt[0] = w_sort(0)
         for q in range(WQ):
+            if W_SORTED and q + 1 < WQ:
+                w_srt[q + 1] = w_sort(q + 1)
             for g in range(G):
                 tp = psum.tile([P, 2, 2, P], F32, name="ps")
                 for t in range(2):
                     words = w_raw[q][:, t, :].bitcast(F32)
                     for u in range(2):
-                        nc.tensor.transpose(tp[:, t, u, :], words[:, 256 * g + u:256 * (g + 1):2], ident[:])
+                        src = w_srt[q][:, t, g, u, :] if W_SORTED else words[:, 256 * g + u:256 * (g + 1):2]
+                        nc.tensor.transpose(tp[:, t, u, :], src, ident[:])
+                if g == G - 1:
+                    for kind, arg in AFTER_W[q]:
+                        if kind == "b":
+                            bias_matmul(arg)
+                        else:
+                            dummy(arg)
                 gr = grp.tile([P, G, P, 4], BF16, name="gr", align_bytes=64)
                 flat = gr[:].rearrange("p a r c -> p (a r c)")
                 nc.scalar.copy(
@@ -113,12 +147,10 @@ def tile_groupfc_kernel(tc, data, W, b, out_0, out_1):
                     scales=w_scales[:, g, cols],
                     in_=flat,
                 )
-
-        for h in range(H):
-            cols = slice(h * 512, (h + 1) * 512)
-            pb = psum.tile([P, 512], F32, name="ps")
-            nc.tensor.matmul(out=pb[:], lhsT=ones[:], rhs=b_row[:, cols], start=True, stop=True)
-            nc.vector.tensor_copy(out=bias[:, cols], in_=pb[:])
+                if g == 0 and len(pbs) > len(bias_done):
+                    h = len(bias_done)
+                    bias_done.append(h)
+                    nc.vector.tensor_copy(out=bias[:, h * 512:(h + 1) * 512], in_=pbs[h][:])
 
         tps = {}
         grs = {}
@@ -230,6 +262,10 @@ def tile_groupfc_kernel(tc, data, W, b, out_0, out_1):
             t_step(i)
         for i in runs[0]:
             e_step(i)
+        while len(bias_done) < H:
+            h = len(bias_done)
+            bias_done.append(h)
+            nc.vector.tensor_copy(out=bias[:, h * 512:(h + 1) * 512], in_=pbs[h][:])
         for i in runs[0]:
             q_step(i)
 

@@ -20,7 +20,7 @@ COPY = mybir.ActivationFunctionType.Copy
 P = 128
 G = 2
 H = 2
-JL = 8
+JL = 16
 J = 4
 NT = B // P
 WQ = 4
@@ -30,9 +30,9 @@ DVE_CAST = 2
 W_SORTED = False
 AFTER_W = ((("b", 0), ("b", 1)), (), (), ())
 LAG = 2
-STORE0 = ((2, 2), (2, 2), (2, 2), (2, 2), (2, 2), (2, 2), (2, 2), (1, 1, 1, 1))
+STORE0 = ((4,), (4,), (4,), (4,), (2, 2), (2, 2), (2, 2), (1, 1, 1, 1))
 STORE1 = ((4,), (4,), (4,), (4,), (4,), (4,), (2, 2), (2, 1, 1))
-FIRST_LOADS = ((0, 2), (2, 4), (4, 8))
+FIRST_LOADS = ((0, 2), (2, 4), (4, 8), (8, 16))
 
 
 def store_width(pattern, j):

@@ -188,17 +188,20 @@ def tile_groupfc_kernel(tc, data, W, b, out_0, out_1):
             for h in range(H):
                 po = psum.tile([P, 512], F32, name="ps")
                 banks.append(po)
-            for g in range(G):
-                for h in range(H):
-                    nc.tensor.matmul_mx(
-                        out=banks[h][:],
-                        lhsT=codes[:, g * P:(g + 1) * P].bitcast(FP8X4),
-                        lhsT_scale=scales[:, g * P:(g + 1) * P],
-                        rhs=w_codes[:, g, h * 512:(h + 1) * 512].bitcast(FP8X4),
-                        rhs_scale=w_scales[:, g, h * 512:(h + 1) * 512],
-                        start=(g == 0),
-                        stop=(g == G - 1),
-                    )
+            if i < NT - 1:
+                order = [(g, h) for g in range(G) for h in range(H)]
+            else:
+                order = [(g, h) for h in range(H) for g in range(G)]
+            for g, h in order:
+                nc.tensor.matmul_mx(
+                    out=banks[h][:],
+                    lhsT=codes[:, g * P:(g + 1) * P].bitcast(FP8X4),
+                    lhsT_scale=scales[:, g * P:(g + 1) * P],
+                    rhs=w_codes[:, g, h * 512:(h + 1) * 512].bitcast(FP8X4),
+                    rhs_scale=w_scales[:, g, h * 512:(h + 1) * 512],
+                    start=(g == 0),
+                    stop=(g == G - 1),
+                )
             pos[i] = banks
 
         def b_step(i):
@@ -209,8 +212,10 @@ def tile_groupfc_kernel(tc, data, W, b, out_0, out_1):
             for h in range(H):
                 cols = slice(h * 512, (h + 1) * 512)
                 nc.vector.tensor_tensor(out=o_t[q][:, j, cols], in0=banks[h][:], in1=bias[:, cols], op=ADD)
+                if i == NT - 1:
+                    nc.sync.dma_start(out=out0_v[i // JL][:, i % JL, cols], in_=o_t[q][:, j, cols])
             w = store_width(STORE0[q], j)
-            if w:
+            if w and i < NT - 1:
                 j8 = i % JL
                 nc.sync.dma_start(out=out0_v[i // JL][:, j8 - w + 1:j8 + 1, :], in_=o_t[q][:, j - w + 1:j + 1, :])
 
@@ -237,7 +242,11 @@ def tile_groupfc_kernel(tc, data, W, b, out_0, out_1):
                     saturate=False,
                 )
             w = store_width(STORE1[q], j)
-            if w:
+            if i == NT - 1:
+                for h in range(H):
+                    cols = slice(h * 512, (h + 1) * 512)
+                    nc.sync.dma_start(out=out1_v[i // JL][:, i % JL, cols], in_=o8_t[q][:, j, cols].bitcast(U8))
+            elif w:
                 j8 = i % JL
                 nc.sync.dma_start(
                     out=out1_v[i // JL][:, j8 - w + 1:j8 + 1, :].rearrange("p j n -> p (j n)"),

from contextlib import ExitStack

import concourse.mybir as mybir
from concourse.masks import make_identity

B, K, N = 4096, 1024, 1024
FLOPS = 2 * B * K * N
Y_SCALE = 340.0

F32 = mybir.dt.float32
BF16 = mybir.dt.bfloat16
U32 = mybir.dt.uint32
U8 = mybir.dt.uint8
FP8X4 = mybir.dt.float8_e4m3fn_x4
FP8 = mybir.dt.float8_e4m3fn
ADD = mybir.AluOpType.add
MULT = mybir.AluOpType.mult
COPY = mybir.ActivationFunctionType.Copy

P = 128
G = 2
H = 2
JL = 16
J = 4
NT = B // P
WQ = 4
WARM = 5
GROUPS = (2,) * 16
DVE_CAST = 2
W_SORTED = False
AFTER_W = ((("b", 0), ("b", 1)), (), (), ())
LAG = 2
STORE0 = ((4,), (4,), (4,), (4,), (2, 2), (2, 2), (2, 2), (1, 1, 1, 1))
STORE1 = ((4,), (4,), (4,), (4,), (4,), (4,), (2, 2), (2, 1, 1))
FIRST_LOADS = ((0, 2), (2, 4), (4, 8), (8, 16))


def store_width(pattern, j):
    first = 0
    for w in pattern:
        if j == first + w - 1:
            return w
        first += w
    return 0


def tile_groupfc_kernel(tc, data, W, b, out_0, out_1):
    nc = tc.nc
    data_v = data.rearrange("(s p j) k -> s p j k", p=P, j=JL)
    out0_v = out_0.rearrange("(s p j) n -> s p j n", p=P, j=JL)
    out1_v = out_1.rearrange("(s p j) n -> s p j n", p=P, j=JL)
    w_v = W.rearrange("(q p t) k -> q p t k", p=P, t=2)

    with ExitStack() as ctx:
        const = ctx.enter_context(tc.tile_pool(name="const", bufs=1))
        raw = ctx.enter_context(tc.tile_pool(name="raw", bufs=1))
        grp = ctx.enter_context(tc.tile_pool(name="grp", bufs=6))
        cod = ctx.enter_context(tc.tile_pool(name="cod", bufs=10))
        outp = ctx.enter_context(tc.tile_pool(name="outp", bufs=4))
        out8 = ctx.enter_context(tc.tile_pool(name="out8", bufs=3))
        psum = ctx.enter_context(tc.psum_pool(name="psum", bufs=8))

        ident = const.tile([P, P], F32, name="ident")
        make_identity(nc, ident[:])
        ones = const.tile([P, P], BF16, name="ones")
        warm = const.tile([P, 512], BF16, name="warm")
        b_row = const.tile([P, N], BF16, name="b_row")
        bias = const.tile([P, N], F32, name="bias")
        w_codes = const.tile([P, G, N], U32, name="w_codes", align_bytes=64)
        w_scales = const.tile([P, G, N], U8, name="w_scales", align_bytes=64)

        ctx.enter_context(tc.manual_schedule())

        nc.vector.memset(b_row[:].bitcast(F32), 0.0)
        nc.vector.memset(ones[:], 1.0)
        nc.vector.memset(warm[:].bitcast(F32), 0.0)

        w_raw = []
        for q in range(WQ):
            wr = raw.tile([P, 2, K], BF16, name="w_raw%d" % q)
            nc.sync.dma_start(out=wr[:], in_=w_v[q])
            w_raw.append(wr)
            if q == 0:
                nc.sync.dma_start(out=b_row[0:1, :], in_=b.rearrange("(o n) -> o n", o=1))
        x_raw = []
        for s in range(NT // JL):
            xr = raw.tile([P, JL, K], BF16, name="x_raw%d" % s)
            x_raw.append(xr)
            if s == 0:
                for j0, j1 in FIRST_LOADS:
                    nc.sync.dma_start(out=xr[:, j0:j1, :], in_=data_v[0][:, j0:j1, :])
            else:
                nc.sync.dma_start(out=xr[:], in_=data_v[s])

        pw = psum.tile([P, 512], F32, name="ps")
        for n in range(WARM):
            nc.tensor.matmul(out=pw[:], lhsT=ones[:], rhs=warm[:], start=True, stop=True)

        def w_sort(q):
            ws = raw.tile([P, 2, G, 2, P], F32, name="w_srt%d" % q)
            nc.vector.tensor_copy(
                out=ws[:].rearrange("p t g u w -> p (t g) u w"),
                in_=w_raw[q][:].rearrange("p t k -> p (t k)").bitcast(F32).rearrange("p (m w u) -> p m u w", m=2 * G, u=2),
            )
            return ws

        def dummy(width):
            pd = psum.tile([P, 512], F32, name="ps")
            nc.tensor.matmul(out=pd[:, :width], lhsT=ones[:], rhs=warm[:, :width], start=True, stop=True)

        pbs = []
        bias_done = []

        def bias_matmul(h):
            pb = psum.tile([P, 512], F32, name="ps")
            nc.tensor.matmul(out=pb[:], lhsT=ones[:], rhs=b_row[:, h * 512:(h + 1) * 512], start=True, stop=True)
            pbs.append(pb)

        w_srt = {}
        if W_SORTED:
            w_srt[0] = w_sort(0)
        for q in range(WQ):
            if W_SORTED and q + 1 < WQ:
                w_srt[q + 1] = w_sort(q + 1)
            for g in range(G):
                tp = psum.tile([P, 2, 2, P], F32, name="ps")
                for t in range(2):
                    words = w_raw[q][:, t, :].bitcast(F32)
                    for u in range(2):
                        src = w_srt[q][:, t, g, u, :] if W_SORTED else words[:, 256 * g + u:256 * (g + 1):2]
                        nc.tensor.transpose(tp[:, t, u, :], src, ident[:])
                if g == G - 1:
                    for kind, arg in AFTER_W[q]:
                        if kind == "b":
                            bias_matmul(arg)
                        else:
                            dummy(arg)
                gr = grp.tile([P, G, P, 4], BF16, name="gr", align_bytes=64)
                flat = gr[:].rearrange("p a r c -> p (a r c)")
                nc.scalar.copy(
                    out=flat.bitcast(F32).rearrange("p (r t u) -> p r t u", t=2, u=2),
                    in_=tp[:].rearrange("p t u r -> p r t u"),
                )
                cols = slice(q * 256, (q + 1) * 256)
                nc.vector.quantize_mx(
                    out=w_codes[:, g, cols].bitcast(FP8X4),
                    scales=w_scales[:, g, cols],
                    in_=flat,
                )
                if g == 0 and len(pbs) > len(bias_done):
                    h = len(bias_done)
                    bias_done.append(h)
                    nc.vector.tensor_copy(out=bias[:, h * 512:(h + 1) * 512], in_=pbs[h][:])

        tps = {}
        grs = {}
        cds = {}
        pos = {}
        o_t = {}
        o8_t = {}

        def t_step(i):
            words = x_raw[i // JL][:, i % JL, :].bitcast(F32)
            tp = psum.tile([P, G, 2, P], F32, name="ps")
            for g in range(G):
                for u in range(2):
                    nc.tensor.transpose(tp[:, g, u, :], words[:, 256 * g + u:256 * (g + 1):2], ident[:])
            tps[i] = tp

        def e_step(i):
            gr = grp.tile([P, G, P, 4], BF16, name="gr", align_bytes=64)
            nc.scalar.copy(out=gr[:].bitcast(F32), in_=tps.pop(i)[:].rearrange("p g u r -> p g r u"))
            grs[i] = gr

        def q_step(i):
            codes = cod.tile([P, G * P], U32, name="codes", align_bytes=64)
            scales = cod.tile([P, G * P], U8, name="scales", align_bytes=64)
            nc.vector.quantize_mx(
                out=codes[:].bitcast(FP8X4),
                scales=scales[:],
                in_=grs.pop(i)[:].rearrange("p g r t -> p (g r t)"),
            )
            cds[i] = (codes, scales)

        def m_step(i):
            codes, scales = cds.pop(i)
            banks = []
            for h in range(H):
                po = psum.tile([P, 512], F32, name="ps")
                banks.append(po)
            if i < NT - 1:
                order = [(g, h) for g in range(G) for h in range(H)]
            else:
                order = [(g, h) for h in range(H) for g in range(G)]
            for g, h in order:
                nc.tensor.matmul_mx(
                    out=banks[h][:],
                    lhsT=codes[:, g * P:(g + 1) * P].bitcast(FP8X4),
                    lhsT_scale=scales[:, g * P:(g + 1) * P],
                    rhs=w_codes[:, g, h * 512:(h + 1) * 512].bitcast(FP8X4),
                    rhs_scale=w_scales[:, g, h * 512:(h + 1) * 512],
                    start=(g == 0),
                    stop=(g == G - 1),
                )
            pos[i] = banks

        def b_step(i):
            q, j = i // J, i % J
            if j == 0:
                o_t[q] = outp.tile([P, J, N], F32, name="o")
            banks = pos.pop(i)
            for h in range(H):
                cols = slice(h * 512, (h + 1) * 512)
                nc.vector.tensor_tensor(out=o_t[q][:, j, cols], in0=banks[h][:], in1=bias[:, cols], op=ADD)
                if i == NT - 1:
                    nc.sync.dma_start(out=out0_v[i // JL][:, i % JL, cols], in_=o_t[q][:, j, cols])
            w = store_width(STORE0[q], j)
            if w and i < NT - 1:
                j8 = i % JL
                nc.sync.dma_start(out=out0_v[i // JL][:, j8 - w + 1:j8 + 1, :], in_=o_t[q][:, j - w + 1:j + 1, :])

        def c_step(i):
            q, j = i // J, i % J
            if j == 0:
                o8_t[q] = out8.tile([P, J, N], FP8, name="o8")
            scalar_cols = 0 if i % J == DVE_CAST else 512 if i == NT - 1 else N
            if scalar_cols:
                nc.scalar.activation(
                    out=o8_t[q][:, j, :scalar_cols],
                    in_=o_t[q][:, j, :scalar_cols],
                    func=COPY,
                    scale=Y_SCALE,
                    saturate=False,
                )
            if scalar_cols < N:
                nc.vector.tensor_scalar(
                    out=o8_t[q][:, j, scalar_cols:],
                    in0=o_t[q][:, j, scalar_cols:],
                    scalar1=Y_SCALE,
                    scalar2=None,
                    op0=MULT,
                    saturate=False,
                )
            w = store_width(STORE1[q], j)
            if i == NT - 1:
                for h in range(H):
                    cols = slice(h * 512, (h + 1) * 512)
                    nc.sync.dma_start(out=out1_v[i // JL][:, i % JL, cols], in_=o8_t[q][:, j, cols].bitcast(U8))
            elif w:
                j8 = i % JL
                nc.sync.dma_start(
                    out=out1_v[i // JL][:, j8 - w + 1:j8 + 1, :].rearrange("p j n -> p (j n)"),
                    in_=o8_t[q][:, j - w + 1:j + 1, :].rearrange("p j n -> p (j n)").bitcast(U8),
                )

        casts = [0]

        def casts_to(last):
            while casts[0] <= last:
                c_step(casts[0])
                casts[0] += 1

        runs = []
        first = 0
        for size in GROUPS:
            runs.append(list(range(first, first + size)))
            first += size
        runs.append([])

        for i in runs[0]:
            t_step(i)
        for i in runs[0]:
            e_step(i)
        while len(bias_done) < H:
            h = len(bias_done)
            bias_done.append(h)
            nc.vector.tensor_copy(out=bias[:, h * 512:(h + 1) * 512], in_=pbs[h][:])
        for i in runs[0]:
            q_step(i)

        for r in range(len(GROUPS)):
            cur = runs[r]
            nxt = runs[r + 1]
            for i in nxt:
                t_step(i)
            for i in nxt:
                e_step(i)
            casts_to(cur[0] - 1)
            for i in nxt:
                q_step(i)
            held = LAG if nxt else 0
            for i in cur:
                m_step(i)
                if i > cur[0]:
                    b_step(i - 1)
                    casts_to(min(i - 1, cur[-1] - held))
            b_step(cur[-1])
        casts_to(NT - 1)
